import numpy as np
import ml_dtypes


def mxq(x, axis, fmt="e4m3"):
    dtype, down = {"e4m3": (ml_dtypes.float8_e4m3fn, 7), "e5m2": (ml_dtypes.float8_e5m2, 14)}[fmt]
    v = np.moveaxis(np.asarray(x, np.float32).astype(ml_dtypes.bfloat16).astype(np.float64), axis, -1)
    blocks = v.reshape(v.shape[:-1] + (-1, 32))
    amax = np.abs(blocks).max(-1, keepdims=True)
    byte = np.maximum(np.where(amax > 0, np.frexp(amax)[1] - 1 + 127, 0) - down, 1)
    scale = np.exp2(byte - 127.0)
    codes = (blocks / scale).astype(np.float32).astype(dtype).astype(np.float64)
    return np.moveaxis((codes * scale).reshape(v.shape), -1, axis)


WIDE = False


def mx_kscale(k):
    if not WIDE:
        return np.ones(k)
    levels = np.array([10, -10, 5, -5, 0])
    a = np.random.permutation(np.resize(levels, k // 512 * 4)).reshape(k // 512, 4)
    idx = np.arange(k)
    return np.exp2(a[idx // 512, idx % 128 // 32])


BF16 = ml_dtypes.bfloat16


def bf(x):
    return np.asarray(x, np.float32).astype(BF16)


def f64(x):
    return np.asarray(x).astype(np.float64)


B, D_IN, D_FEAT, N_EX, N_LAB = 1024, 512, 512, 8192, 128
P_FACTOR = 3.0
EPS = 1e-12


def unit_rows(x):
    return x / np.sqrt((x * x).sum(-1, keepdims=True))


def l1_normalize(x):
    n = np.abs(x).sum(-1, keepdims=True)
    return x / np.maximum(n, EPS)


def setup_inputs():
    s = mx_kscale(D_FEAT)
    return {"f_norm": bf(unit_rows(np.random.standard_normal((B, D_FEAT))) * s),
            "e_norm": bf(unit_rows(np.random.standard_normal((N_EX, D_FEAT))) / s),
            "ex_class_reps": bf(np.random.standard_normal((N_EX, N_LAB)) * 0.0625 * np.sqrt(N_EX))}


def reference(f_norm, e_norm, ex_class_reps):
    s = mxq(f64(f_norm), 1, "e4m3") @ mxq(f64(e_norm), 1, "e4m3").T
    a = np.sign(s) * np.abs(s) ** P_FACTOR
    a = l1_normalize(a)
    return mxq(a, 1, "e4m3") @ mxq(f64(ex_class_reps), 0, "e4m3")

@@ -1,0 +1,209 @@
+import concourse.mybir as mybir
+from concourse.masks import make_identity
+
+F32 = mybir.dt.float32
+BF16 = mybir.dt.bfloat16
+U32 = mybir.dt.uint32
+U8 = mybir.dt.uint8
+FP8X4 = mybir.dt.float8_e4m3fn_x4
+ACT = mybir.ActivationFunctionType
+ALU = mybir.AluOpType
+
+P = 128
+PACK = 4
+K_PASS = P * PACK
+
+QUERIES, FEATURES, EXEMPLARS, LABELS = 1024, 512, 8192, 128
+EPS = 1e-12
+FLOPS = 2 * QUERIES * EXEMPLARS * (FEATURES + LABELS)
+
+Q_TILES = QUERIES // P
+PASSES = EXEMPLARS // K_PASS
+CHUNK = 4
+CHUNK_COLS = CHUNK * K_PASS
+CHUNKS_PER_TILE = PASSES // CHUNK
+N_CHUNKS = Q_TILES * CHUNKS_PER_TILE
+LAG = CHUNKS_PER_TILE + 1
+
+
+def tile_minerva_pa_kernel(tc, f_norm, e_norm, ex_class_reps, out):
+    nc = tc.nc
+    with (
+        tc.tile_pool(name="keep", bufs=1) as keep,
+        tc.tile_pool(name="raw", bufs=8) as raw_pool,
+        tc.tile_pool(name="stage", bufs=3) as stage,
+        tc.tile_pool(name="cubes", bufs=LAG + 2) as cubes,
+        tc.tile_pool(name="small", bufs=3) as small,
+        tc.psum_pool(name="psum_s", bufs=4) as psum_s,
+        tc.psum_pool(name="psum_flip", bufs=3) as psum_flip,
+        tc.psum_pool(name="psum_echo", bufs=1) as psum_echo,
+    ):
+        f_raw, e_raw, r_raw = [], [], []
+        for h in range(QUERIES // K_PASS):
+            raw = raw_pool.tile([P, PACK * FEATURES], BF16, tag="raw")
+            nc.sync.dma_start(
+                out=raw[:].rearrange("p (j k) -> p j k", j=PACK),
+                in_=f_norm[h * K_PASS : (h + 1) * K_PASS, :].rearrange("(j p) k -> p j k", p=P),
+            )
+            f_raw.append(raw)
+        for c in range(PASSES):
+            raw = raw_pool.tile([P, PACK * FEATURES], BF16, tag="raw")
+            nc.sync.dma_start(
+                out=raw[:],
+                in_=e_norm[c * K_PASS : (c + 1) * K_PASS, :].rearrange("(p t) k -> p (t k)", t=PACK),
+            )
+            e_raw.append(raw)
+        for g in range(CHUNKS_PER_TILE):
+            raw = raw_pool.tile([P, CHUNK * PACK * LABELS], BF16, tag="raw")
+            nc.sync.dma_start(
+                out=raw[:].rearrange("p (c x) -> p c x", c=CHUNK),
+                in_=ex_class_reps[g * CHUNK_COLS : (g + 1) * CHUNK_COLS, :].rearrange(
+                    "(c p t) n -> p c (t n)", p=P, t=PACK
+                ),
+            )
+            r_raw.append(raw)
+
+        ident = keep.tile([P, P], F32)
+        make_identity(nc, ident[:])
+        ones = keep.tile([P, P], F32)
+        nc.vector.memset(ones[:], 1.0)
+
+        f_codes = keep.tile([P, QUERIES], U32, align_bytes=64)
+        f_scales = keep.tile([P, QUERIES], U8, align_bytes=64)
+        e_codes = keep.tile([P, EXEMPLARS], U32, align_bytes=64)
+        e_scales = keep.tile([P, EXEMPLARS], U8, align_bytes=64)
+        r_codes = keep.tile([P, PASSES * LABELS], U32, align_bytes=64)
+        r_scales = keep.tile([P, PASSES * LABELS], U8, align_bytes=64)
+        abs_out = keep.tile([P, CHUNK_COLS], BF16)
+
+        def quantise_along_features(raw, codes, scales):
+            words = raw[:].bitcast(F32)
+            grouped = stage.tile([P, K_PASS * PACK], BF16, tag="grouped", align_bytes=64)
+            grouped_words = grouped[:].bitcast(F32).rearrange("p (j r u) -> p j r u", j=PACK, u=2)
+            for half in range(2):
+                flipped = psum_flip.tile([P, PACK, P], F32, tag="flipped")
+                for j in range(2):
+                    for u in range(2):
+                        first = (2 * half + j) * (FEATURES // 2) + u * P
+                        nc.tensor.transpose(flipped[:, 2 * j + u, :], words[:, first : first + P], ident[:])
+                source = flipped[:].rearrange("p (j u) r -> p j r u", u=2)
+                target = grouped_words[:, 2 * half : 2 * half + 2, :, :]
+                if half == 0:
+                    nc.scalar.copy(out=target, in_=source)
+                else:
+                    nc.vector.tensor_copy(out=target, in_=source)
+            nc.vector.quantize_mx(out=codes.bitcast(FP8X4), scales=scales, in_=grouped[:])
+
+        def quantise_class_reps(g):
+            grouped = stage.tile([P, CHUNK * LABELS * PACK], BF16, tag="grouped", align_bytes=64)
+            nc.vector.tensor_copy(
+                out=grouped[:].rearrange("p (c n t) -> p c n t", c=CHUNK, t=PACK),
+                in_=r_raw[g][:].rearrange("p (c t n) -> p c n t", c=CHUNK, t=PACK),
+            )
+            cols = slice(g * CHUNK * LABELS, (g + 1) * CHUNK * LABELS)
+            nc.vector.quantize_mx(out=r_codes[:, cols].bitcast(FP8X4), scales=r_scales[:, cols], in_=grouped[:])
+
+        a_chunks, abs_sums, recip_rows, p_groups, echoes = {}, {}, {}, {}, {}
+
+        def similarities_cubed(m):
+            i, g = divmod(m, CHUNKS_PER_TILE)
+            a_chunk = cubes.tile([P, CHUNK_COLS], F32, tag="a_chunk")
+            a_chunks[m] = a_chunk
+            for cc in range(CHUNK):
+                e_cols = slice((g * CHUNK + cc) * K_PASS, (g * CHUNK + cc + 1) * K_PASS)
+                q_cols = slice(i * P, (i + 1) * P)
+                s = psum_s.tile([P, K_PASS], F32, tag="s")
+                nc.tensor.matmul_mx(
+                    out=s[:],
+                    lhsT=f_codes[:, q_cols].bitcast(FP8X4),
+                    lhsT_scale=f_scales[:, q_cols],
+                    rhs=e_codes[:, e_cols].bitcast(FP8X4),
+                    rhs_scale=e_scales[:, e_cols],
+                    start=True,
+                    stop=True,
+                )
+                squared = stage.tile([P, K_PASS], F32, tag="squared")
+                nc.scalar.activation(out=squared[:], in_=s[:], func=ACT.Square)
+                nc.vector.tensor_tensor(
+                    out=a_chunk[:, cc * K_PASS : (cc + 1) * K_PASS], in0=s[:], in1=squared[:], op=ALU.mult
+                )
+            if g == 0:
+                abs_sum = small.tile([P, CHUNKS_PER_TILE], F32, tag="abs_sum")
+                abs_sums[i] = abs_sum
+            nc.scalar.activation(out=abs_out[:], in_=a_chunk[:], func=ACT.Abs, accum_out=abs_sums[i][:, g : g + 1])
+
+        def reciprocal_of_row_sum(i):
+            total = small.tile([P, 1], F32, tag="total")
+            nc.vector.reduce_sum(out=total[:], in_=abs_sums[i][:], axis=mybir.AxisListType.X)
+            nc.vector.tensor_scalar_max(out=total[:], in0=total[:], scalar1=EPS)
+            recip = small.tile([P, 1], F32, tag="recip")
+            nc.vector.reciprocal(out=recip[:], in_=total[:])
+            spread = small.tile([P, P], F32, tag="spread")
+            nc.vector.tensor_scalar_mul(out=spread[:], in0=ones[:], scalar1=recip[:, 0:1])
+            flipped = psum_flip.tile([P, PACK, P], F32, tag="flipped")
+            nc.tensor.transpose(flipped[:, 0, :], spread[:], ident[:])
+            recip_row = small.tile([P, P], F32, tag="recip_row")
+            nc.vector.tensor_copy(out=recip_row[:], in_=flipped[:, 0, :])
+            recip_rows[i] = recip_row
+
+        def normalise_and_transpose(m):
+            i = m // CHUNKS_PER_TILE
+            p_group = stage.tile([P, CHUNK * P * PACK], BF16, tag="p_group", align_bytes=64)
+            p_groups[m] = p_group
+            for cc in range(CHUNK):
+                flipped = psum_flip.tile([P, PACK, P], F32, tag="flipped")
+                for t in range(PACK):
+                    first = cc * K_PASS + t * P
+                    nc.tensor.transpose(flipped[:, t, :], a_chunks[m][:, first : first + P], ident[:])
+                nc.vector.tensor_tensor(
+                    out=p_group[:, cc * K_PASS : (cc + 1) * K_PASS].rearrange("p (q t) -> p q t", t=PACK),
+                    in0=flipped[:].rearrange("p t q -> p q t"),
+                    in1=recip_rows[i][:].unsqueeze(2).to_broadcast([P, P, PACK]),
+                    op=ALU.mult,
+                )
+
+        def quantise_and_read_out(m):
+            i, g = divmod(m, CHUNKS_PER_TILE)
+            p_codes = stage.tile([P, CHUNK * P], U32, tag="p_codes", align_bytes=64)
+            p_scales = stage.tile([P, CHUNK * P], U8, tag="p_scales", align_bytes=64)
+            nc.vector.quantize_mx(out=p_codes[:].bitcast(FP8X4), scales=p_scales[:], in_=p_groups[m][:])
+            if g == 0:
+                echo = psum_echo.tile([P, LABELS], F32, tag="echo")
+                echoes[i] = echo
+            for cc in range(CHUNK):
+                c = g * CHUNK + cc
+                q_cols = slice(cc * P, (cc + 1) * P)
+                n_cols = slice(c * LABELS, (c + 1) * LABELS)
+                nc.tensor.matmul_mx(
+                    out=echoes[i][:],
+                    lhsT=p_codes[:, q_cols].bitcast(FP8X4),
+                    lhsT_scale=p_scales[:, q_cols],
+                    rhs=r_codes[:, n_cols].bitcast(FP8X4),
+                    rhs_scale=r_scales[:, n_cols],
+                    start=(c == 0),
+                    stop=(c == PASSES - 1),
+                )
+            if g == CHUNKS_PER_TILE - 1:
+                result = small.tile([P, LABELS], F32, tag="result")
+                nc.scalar.copy(out=result[:], in_=echoes[i][:])
+                nc.sync.dma_start(out=out[i * P : (i + 1) * P, :], in_=result[:])
+
+        for h in range(QUERIES // K_PASS):
+            cols = slice(h * K_PASS, (h + 1) * K_PASS)
+            quantise_along_features(f_raw[h], f_codes[:, cols], f_scales[:, cols])
+        for step in range(N_CHUNKS + LAG + 1):
+            if step < CHUNKS_PER_TILE:
+                for c in range(step * CHUNK, (step + 1) * CHUNK):
+                    cols = slice(c * K_PASS, (c + 1) * K_PASS)
+                    quantise_along_features(e_raw[c], e_codes[:, cols], e_scales[:, cols])
+            if step == CHUNKS_PER_TILE:
+                for g in range(CHUNKS_PER_TILE):
+                    quantise_class_reps(g)
+            if step < N_CHUNKS:
+                similarities_cubed(step)
+                if step % CHUNKS_PER_TILE == CHUNKS_PER_TILE - 1:
+                    reciprocal_of_row_sum(step // CHUNKS_PER_TILE)
+            if 0 <= step - LAG < N_CHUNKS:
+                normalise_and_transpose(step - LAG)
+            if 0 <= step - LAG - 1 < N_CHUNKS:
+                quantise_and_read_out(step - LAG - 1)

@@ -19,11 +19,12 @@ FLOPS = 2 * QUERIES * EXEMPLARS * (FEATURES + LABELS)
 
 Q_TILES = QUERIES // P
 PASSES = EXEMPLARS // K_PASS
-CHUNK = 4
-CHUNK_COLS = CHUNK * K_PASS
-CHUNKS_PER_TILE = PASSES // CHUNK
-N_CHUNKS = Q_TILES * CHUNKS_PER_TILE
-LAG = CHUNKS_PER_TILE + 1
+PAIR = 2
+PAIR_COLS = PAIR * K_PASS
+PAIRS_PER_TILE = PASSES // PAIR
+N_PAIRS = Q_TILES * PAIRS_PER_TILE
+R_PIECES = 4
+LAG = PAIRS_PER_TILE + 3
 
 
 def tile_minerva_pa_kernel(tc, f_norm, e_norm, ex_class_reps, out):
@@ -32,36 +33,42 @@ def tile_minerva_pa_kernel(tc, f_norm, e_norm, ex_class_reps, out):
         tc.tile_pool(name="keep", bufs=1) as keep,
         tc.tile_pool(name="raw", bufs=8) as raw_pool,
         tc.tile_pool(name="stage", bufs=3) as stage,
-        tc.tile_pool(name="cubes", bufs=LAG + 2) as cubes,
+        tc.tile_pool(name="cubes", bufs=LAG + 1) as cubes,
         tc.tile_pool(name="small", bufs=3) as small,
-        tc.psum_pool(name="psum_s", bufs=4) as psum_s,
+        tc.psum_pool(name="psum_s", bufs=2 * PAIR) as psum_s,
         tc.psum_pool(name="psum_flip", bufs=3) as psum_flip,
         tc.psum_pool(name="psum_echo", bufs=1) as psum_echo,
+        tc.manual_schedule(),
     ):
-        f_raw, e_raw, r_raw = [], [], []
-        for h in range(QUERIES // K_PASS):
+        def load_queries(h):
             raw = raw_pool.tile([P, PACK * FEATURES], BF16, tag="raw")
             nc.sync.dma_start(
                 out=raw[:].rearrange("p (j k) -> p j k", j=PACK),
                 in_=f_norm[h * K_PASS : (h + 1) * K_PASS, :].rearrange("(j p) k -> p j k", p=P),
             )
-            f_raw.append(raw)
-        for c in range(PASSES):
+            return raw
+
+        def load_exemplars(c):
             raw = raw_pool.tile([P, PACK * FEATURES], BF16, tag="raw")
             nc.sync.dma_start(
                 out=raw[:],
                 in_=e_norm[c * K_PASS : (c + 1) * K_PASS, :].rearrange("(p t) k -> p (t k)", t=PACK),
             )
-            e_raw.append(raw)
-        for g in range(CHUNKS_PER_TILE):
-            raw = raw_pool.tile([P, CHUNK * PACK * LABELS], BF16, tag="raw")
+            return raw
+
+        def load_class_reps(g):
+            raw = raw_pool.tile([P, PACK * PACK * LABELS], BF16, tag="raw")
+            rows = ex_class_reps[g * PACK * K_PASS : (g + 1) * PACK * K_PASS, :]
             nc.sync.dma_start(
-                out=raw[:].rearrange("p (c x) -> p c x", c=CHUNK),
-                in_=ex_class_reps[g * CHUNK_COLS : (g + 1) * CHUNK_COLS, :].rearrange(
-                    "(c p t) n -> p c (t n)", p=P, t=PACK
-                ),
+                out=raw[:].rearrange("p (c x) -> p c x", c=PACK),
+                in_=rows.rearrange("(c p t) n -> p c (t n)", p=P, t=PACK),
             )
-            r_raw.append(raw)
+            return raw
+
+        f_raw = [load_queries(0)]
+        e_raw = [load_exemplars(c) for c in range(PASSES)]
+        f_raw.append(load_queries(1))
+        r_raw = [load_class_reps(g) for g in range(R_PIECES)]
 
         ident = keep.tile([P, P], F32)
         make_identity(nc, ident[:])
@@ -74,9 +81,9 @@ def tile_minerva_pa_kernel(tc, f_norm, e_norm, ex_class_reps, out):
         e_scales = keep.tile([P, EXEMPLARS], U8, align_bytes=64)
         r_codes = keep.tile([P, PASSES * LABELS], U32, align_bytes=64)
         r_scales = keep.tile([P, PASSES * LABELS], U8, align_bytes=64)
-        abs_out = keep.tile([P, CHUNK_COLS], BF16)
+        abs_out = keep.tile([P, PAIR_COLS], BF16)
 
-        def quantise_along_features(raw, codes, scales):
+        def features_to_partitions(raw):
             words = raw[:].bitcast(F32)
             grouped = stage.tile([P, K_PASS * PACK], BF16, tag="grouped", align_bytes=64)
             grouped_words = grouped[:].bitcast(F32).rearrange("p (j r u) -> p j r u", j=PACK, u=2)
@@ -92,26 +99,33 @@ def tile_minerva_pa_kernel(tc, f_norm, e_norm, ex_class_reps, out):
                     nc.scalar.copy(out=target, in_=source)
                 else:
                     nc.vector.tensor_copy(out=target, in_=source)
-            nc.vector.quantize_mx(out=codes.bitcast(FP8X4), scales=scales, in_=grouped[:])
+            return grouped
 
-        def quantise_class_reps(g):
-            grouped = stage.tile([P, CHUNK * LABELS * PACK], BF16, tag="grouped", align_bytes=64)
+        def quantise(grouped, codes, scales, first, width):
+            cols = slice(first, first + width)
+            nc.vector.quantize_mx(out=codes[:, cols].bitcast(FP8X4), scales=scales[:, cols], in_=grouped[:])
+
+        def prepare_class_reps(g):
+            grouped = stage.tile([P, PACK * LABELS * PACK], BF16, tag="grouped", align_bytes=64)
             nc.vector.tensor_copy(
-                out=grouped[:].rearrange("p (c n t) -> p c n t", c=CHUNK, t=PACK),
-                in_=r_raw[g][:].rearrange("p (c t n) -> p c n t", c=CHUNK, t=PACK),
+                out=grouped[:].rearrange("p (c n t) -> p c n t", c=PACK, t=PACK),
+                in_=r_raw[g][:].rearrange("p (c t n) -> p c n t", c=PACK, t=PACK),
             )
-            cols = slice(g * CHUNK * LABELS, (g + 1) * CHUNK * LABELS)
-            nc.vector.quantize_mx(out=r_codes[:, cols].bitcast(FP8X4), scales=r_scales[:, cols], in_=grouped[:])
+            return grouped
 
-        a_chunks, abs_sums, recip_rows, p_groups, echoes = {}, {}, {}, {}, {}
+        s_banks, squares, a_pairs, abs_sums, recip_rows, flips, p_groups, p_quantised, echoes = (
+            {}, {}, {}, {}, {}, {}, {}, {}, {},
+        )
 
-        def similarities_cubed(m):
-            i, g = divmod(m, CHUNKS_PER_TILE)
-            a_chunk = cubes.tile([P, CHUNK_COLS], F32, tag="a_chunk")
-            a_chunks[m] = a_chunk
-            for cc in range(CHUNK):
-                e_cols = slice((g * CHUNK + cc) * K_PASS, (g * CHUNK + cc + 1) * K_PASS)
-                q_cols = slice(i * P, (i + 1) * P)
+        def is_pair(j):
+            return 0 <= j < N_PAIRS
+
+        def similarities(j):
+            i, pair = divmod(j, PAIRS_PER_TILE)
+            q_cols = slice(i * P, (i + 1) * P)
+            for cc in range(PAIR):
+                c = pair * PAIR + cc
+                e_cols = slice(c * K_PASS, (c + 1) * K_PASS)
                 s = psum_s.tile([P, K_PASS], F32, tag="s")
                 nc.tensor.matmul_mx(
                     out=s[:],
@@ -122,15 +136,33 @@ def tile_minerva_pa_kernel(tc, f_norm, e_norm, ex_class_reps, out):
                     start=True,
                     stop=True,
                 )
-                squared = stage.tile([P, K_PASS], F32, tag="squared")
-                nc.scalar.activation(out=squared[:], in_=s[:], func=ACT.Square)
+                s_banks[j, cc] = s
+
+        def square(j):
+            for cc in range(PAIR):
+                squared = stage.tile([P, K_PASS], F32, tag="squared", bufs=2 * PAIR)
+                nc.scalar.activation(out=squared[:], in_=s_banks[j, cc][:], func=ACT.Square)
+                squares[j, cc] = squared
+
+        def cube(j):
+            a_pair = cubes.tile([P, PAIR_COLS], F32, tag="a_pair")
+            for cc in range(PAIR):
                 nc.vector.tensor_tensor(
-                    out=a_chunk[:, cc * K_PASS : (cc + 1) * K_PASS], in0=s[:], in1=squared[:], op=ALU.mult
+                    out=a_pair[:, cc * K_PASS : (cc + 1) * K_PASS],
+                    in0=s_banks[j, cc][:],
+                    in1=squares[j, cc][:],
+                    op=ALU.mult,
                 )
-            if g == 0:
-                abs_sum = small.tile([P, CHUNKS_PER_TILE], F32, tag="abs_sum")
+            a_pairs[j] = a_pair
+
+        def sum_of_abs(j):
+            i, pair = divmod(j, PAIRS_PER_TILE)
+            if pair == 0:
+                abs_sum = small.tile([P, PAIRS_PER_TILE], F32, tag="abs_sum")
                 abs_sums[i] = abs_sum
-            nc.scalar.activation(out=abs_out[:], in_=a_chunk[:], func=ACT.Abs, accum_out=abs_sums[i][:, g : g + 1])
+            nc.scalar.activation(
+                out=abs_out[:], in_=a_pairs[j][:], func=ACT.Abs, accum_out=abs_sums[i][:, pair : pair + 1]
+            )
 
         def reciprocal_of_row_sum(i):
             total = small.tile([P, 1], F32, tag="total")
@@ -142,36 +174,47 @@ def tile_minerva_pa_kernel(tc, f_norm, e_norm, ex_class_reps, out):
             nc.vector.tensor_scalar_mul(out=spread[:], in0=ones[:], scalar1=recip[:, 0:1])
             flipped = psum_flip.tile([P, PACK, P], F32, tag="flipped")
             nc.tensor.transpose(flipped[:, 0, :], spread[:], ident[:])
+            return flipped
+
+        def keep_reciprocal_row(i, flipped):
             recip_row = small.tile([P, P], F32, tag="recip_row")
             nc.vector.tensor_copy(out=recip_row[:], in_=flipped[:, 0, :])
             recip_rows[i] = recip_row
 
-        def normalise_and_transpose(m):
-            i = m // CHUNKS_PER_TILE
-            p_group = stage.tile([P, CHUNK * P * PACK], BF16, tag="p_group", align_bytes=64)
-            p_groups[m] = p_group
-            for cc in range(CHUNK):
+        def exemplars_to_partitions(j):
+            for cc in range(PAIR):
                 flipped = psum_flip.tile([P, PACK, P], F32, tag="flipped")
                 for t in range(PACK):
                     first = cc * K_PASS + t * P
-                    nc.tensor.transpose(flipped[:, t, :], a_chunks[m][:, first : first + P], ident[:])
+                    nc.tensor.transpose(flipped[:, t, :], a_pairs[j][:, first : first + P], ident[:])
+                flips[j, cc] = flipped
+
+        def normalise(j):
+            i = j // PAIRS_PER_TILE
+            p_group = stage.tile([P, PAIR * P * PACK], BF16, tag="p_group", align_bytes=64)
+            for cc in range(PAIR):
                 nc.vector.tensor_tensor(
                     out=p_group[:, cc * K_PASS : (cc + 1) * K_PASS].rearrange("p (q t) -> p q t", t=PACK),
-                    in0=flipped[:].rearrange("p t q -> p q t"),
+                    in0=flips[j, cc][:].rearrange("p t q -> p q t"),
                     in1=recip_rows[i][:].unsqueeze(2).to_broadcast([P, P, PACK]),
                     op=ALU.mult,
                 )
+            p_groups[j] = p_group
 
-        def quantise_and_read_out(m):
-            i, g = divmod(m, CHUNKS_PER_TILE)
-            p_codes = stage.tile([P, CHUNK * P], U32, tag="p_codes", align_bytes=64)
-            p_scales = stage.tile([P, CHUNK * P], U8, tag="p_scales", align_bytes=64)
-            nc.vector.quantize_mx(out=p_codes[:].bitcast(FP8X4), scales=p_scales[:], in_=p_groups[m][:])
-            if g == 0:
+        def quantise_p(j):
+            p_codes = stage.tile([P, PAIR * P], U32, tag="p_codes", align_bytes=64)
+            p_scales = stage.tile([P, PAIR * P], U8, tag="p_scales", align_bytes=64)
+            quantise(p_groups[j], p_codes, p_scales, 0, PAIR * P)
+            p_quantised[j] = (p_codes, p_scales)
+
+        def read_out(j):
+            i, pair = divmod(j, PAIRS_PER_TILE)
+            p_codes, p_scales = p_quantised[j]
+            if pair == 0:
                 echo = psum_echo.tile([P, LABELS], F32, tag="echo")
                 echoes[i] = echo
-            for cc in range(CHUNK):
-                c = g * CHUNK + cc
+            for cc in range(PAIR):
+                c = pair * PAIR + cc
                 q_cols = slice(cc * P, (cc + 1) * P)
                 n_cols = slice(c * LABELS, (c + 1) * LABELS)
                 nc.tensor.matmul_mx(
@@ -183,27 +226,46 @@ def tile_minerva_pa_kernel(tc, f_norm, e_norm, ex_class_reps, out):
                     start=(c == 0),
                     stop=(c == PASSES - 1),
                 )
-            if g == CHUNKS_PER_TILE - 1:
+            if pair == PAIRS_PER_TILE - 1:
                 result = small.tile([P, LABELS], F32, tag="result")
                 nc.scalar.copy(out=result[:], in_=echoes[i][:])
                 nc.sync.dma_start(out=out[i * P : (i + 1) * P, :], in_=result[:])
 
-        for h in range(QUERIES // K_PASS):
-            cols = slice(h * K_PASS, (h + 1) * K_PASS)
-            quantise_along_features(f_raw[h], f_codes[:, cols], f_scales[:, cols])
-        for step in range(N_CHUNKS + LAG + 1):
-            if step < CHUNKS_PER_TILE:
-                for c in range(step * CHUNK, (step + 1) * CHUNK):
-                    cols = slice(c * K_PASS, (c + 1) * K_PASS)
-                    quantise_along_features(e_raw[c], e_codes[:, cols], e_scales[:, cols])
-            if step == CHUNKS_PER_TILE:
-                for g in range(CHUNKS_PER_TILE):
-                    quantise_class_reps(g)
-            if step < N_CHUNKS:
-                similarities_cubed(step)
-                if step % CHUNKS_PER_TILE == CHUNKS_PER_TILE - 1:
-                    reciprocal_of_row_sum(step // CHUNKS_PER_TILE)
-            if 0 <= step - LAG < N_CHUNKS:
-                normalise_and_transpose(step - LAG)
-            if 0 <= step - LAG - 1 < N_CHUNKS:
-                quantise_and_read_out(step - LAG - 1)
+        grouped = features_to_partitions(f_raw[0])
+        quantise(grouped, f_codes, f_scales, 0, K_PASS)
+        spread_flipped = {}
+        for tick in range(-3, N_PAIRS + LAG + 1):
+            prepared = []
+            if tick + 3 < PAIRS_PER_TILE:
+                for c in range((tick + 3) * PAIR, (tick + 4) * PAIR):
+                    prepared.append((features_to_partitions(e_raw[c]), e_codes, e_scales, c * K_PASS))
+            elif tick + 3 == PAIRS_PER_TILE:
+                prepared.append((features_to_partitions(f_raw[1]), f_codes, f_scales, K_PASS))
+            elif tick + 3 <= PAIRS_PER_TILE + R_PIECES:
+                g = tick + 3 - PAIRS_PER_TILE - 1
+                prepared.append((prepare_class_reps(g), r_codes, r_scales, g * K_PASS))
+
+            if is_pair(tick + 1):
+                square(tick + 1)
+            if is_pair(tick - 1):
+                sum_of_abs(tick - 1)
+            if is_pair(tick):
+                cube(tick)
+            for grouped, codes, scales, first in prepared:
+                quantise(grouped, codes, scales, first, K_PASS)
+            if is_pair(tick - LAG - 1):
+                quantise_p(tick - LAG - 1)
+            if is_pair(tick - PAIRS_PER_TILE - 2) and (tick - 2) % PAIRS_PER_TILE == 0:
+                i = (tick - 2) // PAIRS_PER_TILE - 1
+                keep_reciprocal_row(i, spread_flipped[i])
+            if is_pair(tick - LAG):
+                normalise(tick - LAG)
+            if is_pair(tick + 2):
+                similarities(tick + 2)
+            if is_pair(tick - LAG - 1):
+                read_out(tick - LAG - 1)
+            if is_pair(tick - PAIRS_PER_TILE - 1) and (tick - 1) % PAIRS_PER_TILE == 0:
+                i = (tick - 1) // PAIRS_PER_TILE - 1
+                spread_flipped[i] = reciprocal_of_row_sum(i)
+            if is_pair(tick - LAG + 1):
+                exemplars_to_partitions(tick - LAG + 1)

@@ -23,7 +23,9 @@ PAIR = 2
 PAIR_COLS = PAIR * K_PASS
 PAIRS_PER_TILE = PASSES // PAIR
 N_PAIRS = Q_TILES * PAIRS_PER_TILE
+QUAD = 2
 R_PIECES = 4
+SCALAR_EVERY = 8
 LAG = PAIRS_PER_TILE + 3
 
 
@@ -113,12 +115,15 @@ def tile_minerva_pa_kernel(tc, f_norm, e_norm, ex_class_reps, out):
             )
             return grouped
 
-        s_banks, squares, a_pairs, abs_sums, recip_rows, flips, p_groups, p_quantised, echoes = (
-            {}, {}, {}, {}, {}, {}, {}, {}, {},
+        s_banks, squares, a_pairs, abs_sums, totals, recips, recip_rows, flips, p_groups, echoes = (
+            {}, {}, {}, {}, {}, {}, {}, {}, {}, {},
         )
 
         def is_pair(j):
             return 0 <= j < N_PAIRS
+
+        def scalar_way(j, cc):
+            return (j * PAIR + cc) % SCALAR_EVERY == SCALAR_EVERY - 1
 
         def similarities(j):
             i, pair = divmod(j, PAIRS_PER_TILE)
@@ -163,23 +168,37 @@ def tile_minerva_pa_kernel(tc, f_norm, e_norm, ex_class_reps, out):
             nc.scalar.activation(
                 out=abs_out[:], in_=a_pairs[j][:], func=ACT.Abs, accum_out=abs_sums[i][:, pair : pair + 1]
             )
+            if pair == PAIRS_PER_TILE - 1:
+                total = small.tile([P, 1], F32, tag="total")
+                nc.scalar.activation(
+                    out=abs_out[:, 0:PAIRS_PER_TILE], in_=abs_sums[i][:], func=ACT.Copy, accum_out=total[:]
+                )
+                totals[i] = total
 
         def reciprocal_of_row_sum(i):
-            total = small.tile([P, 1], F32, tag="total")
-            nc.vector.reduce_sum(out=total[:], in_=abs_sums[i][:], axis=mybir.AxisListType.X)
-            nc.vector.tensor_scalar_max(out=total[:], in0=total[:], scalar1=EPS)
             recip = small.tile([P, 1], F32, tag="recip")
-            nc.vector.reciprocal(out=recip[:], in_=total[:])
+            nc.vector.tensor_scalar_max(out=recip[:], in0=totals[i][:], scalar1=EPS)
+            nc.vector.reciprocal(out=recip[:], in_=recip[:])
+            recips[i] = recip
             spread = small.tile([P, P], F32, tag="spread")
-            nc.vector.tensor_scalar_mul(out=spread[:], in0=ones[:], scalar1=recip[:, 0:1])
+            nc.scalar.activation(out=spread[:], in_=ones[:], func=ACT.Copy, scale=recip[:, 0:1])
             flipped = psum_flip.tile([P, PACK, P], F32, tag="flipped")
             nc.tensor.transpose(flipped[:, 0, :], spread[:], ident[:])
             return flipped
 
         def keep_reciprocal_row(i, flipped):
             recip_row = small.tile([P, P], F32, tag="recip_row")
-            nc.vector.tensor_copy(out=recip_row[:], in_=flipped[:, 0, :])
+            nc.scalar.copy(out=recip_row[:], in_=flipped[:, 0, :])
             recip_rows[i] = recip_row
+
+        def normalise_before_transposes(j):
+            i = j // PAIRS_PER_TILE
+            for cc in range(PAIR):
+                if scalar_way(j, cc):
+                    a_pass = a_pairs[j][:, cc * K_PASS : (cc + 1) * K_PASS]
+                    nc.gpsimd.tensor_scalar(
+                        out=a_pass, in0=a_pass, scalar1=recips[i][:, 0:1], scalar2=0.0, op0=ALU.mult, op1=ALU.add
+                    )
 
         def exemplars_to_partitions(j):
             for cc in range(PAIR):
@@ -191,30 +210,34 @@ def tile_minerva_pa_kernel(tc, f_norm, e_norm, ex_class_reps, out):
 
         def normalise(j):
             i = j // PAIRS_PER_TILE
-            p_group = stage.tile([P, PAIR * P * PACK], BF16, tag="p_group", align_bytes=64)
+            if j % QUAD == 0:
+                p_group = stage.tile([P, QUAD * PAIR * P * PACK], BF16, tag="p_group", align_bytes=64)
+                p_groups[j // QUAD] = p_group
             for cc in range(PAIR):
-                nc.vector.tensor_tensor(
-                    out=p_group[:, cc * K_PASS : (cc + 1) * K_PASS].rearrange("p (q t) -> p q t", t=PACK),
-                    in0=flips[j, cc][:].rearrange("p t q -> p q t"),
-                    in1=recip_rows[i][:].unsqueeze(2).to_broadcast([P, P, PACK]),
-                    op=ALU.mult,
-                )
-            p_groups[j] = p_group
+                first = ((j % QUAD) * PAIR + cc) * K_PASS
+                target = p_groups[j // QUAD][:, first : first + K_PASS].rearrange("p (q t) -> p q t", t=PACK)
+                source = flips[j, cc][:].rearrange("p t q -> p q t")
+                if scalar_way(j, cc):
+                    nc.scalar.copy(out=target, in_=source)
+                else:
+                    nc.vector.tensor_tensor(
+                        out=target,
+                        in0=source,
+                        in1=recip_rows[i][:].unsqueeze(2).to_broadcast([P, P, PACK]),
+                        op=ALU.mult,
+                    )
 
-        def quantise_p(j):
-            p_codes = stage.tile([P, PAIR * P], U32, tag="p_codes", align_bytes=64)
-            p_scales = stage.tile([P, PAIR * P], U8, tag="p_scales", align_bytes=64)
-            quantise(p_groups[j], p_codes, p_scales, 0, PAIR * P)
-            p_quantised[j] = (p_codes, p_scales)
-
-        def read_out(j):
-            i, pair = divmod(j, PAIRS_PER_TILE)
-            p_codes, p_scales = p_quantised[j]
-            if pair == 0:
+        def read_out(quad):
+            passes = QUAD * PAIR
+            i, part = divmod(quad, PASSES // passes)
+            p_codes = stage.tile([P, passes * P], U32, tag="p_codes", align_bytes=64)
+            p_scales = stage.tile([P, passes * P], U8, tag="p_scales", align_bytes=64)
+            quantise(p_groups[quad], p_codes, p_scales, 0, passes * P)
+            if part == 0:
                 echo = psum_echo.tile([P, LABELS], F32, tag="echo")
                 echoes[i] = echo
-            for cc in range(PAIR):
-                c = pair * PAIR + cc
+            for cc in range(passes):
+                c = part * passes + cc
                 q_cols = slice(cc * P, (cc + 1) * P)
                 n_cols = slice(c * LABELS, (c + 1) * LABELS)
                 nc.tensor.matmul_mx(
@@ -226,7 +249,7 @@ def tile_minerva_pa_kernel(tc, f_norm, e_norm, ex_class_reps, out):
                     start=(c == 0),
                     stop=(c == PASSES - 1),
                 )
-            if pair == PAIRS_PER_TILE - 1:
+            if c == PASSES - 1:
                 result = small.tile([P, LABELS], F32, tag="result")
                 nc.scalar.copy(out=result[:], in_=echoes[i][:])
                 nc.sync.dma_start(out=out[i * P : (i + 1) * P, :], in_=result[:])
@@ -253,19 +276,19 @@ def tile_minerva_pa_kernel(tc, f_norm, e_norm, ex_class_reps, out):
                 cube(tick)
             for grouped, codes, scales, first in prepared:
                 quantise(grouped, codes, scales, first, K_PASS)
-            if is_pair(tick - LAG - 1):
-                quantise_p(tick - LAG - 1)
             if is_pair(tick - PAIRS_PER_TILE - 2) and (tick - 2) % PAIRS_PER_TILE == 0:
                 i = (tick - 2) // PAIRS_PER_TILE - 1
                 keep_reciprocal_row(i, spread_flipped[i])
-            if is_pair(tick - LAG):
-                normalise(tick - LAG)
             if is_pair(tick + 2):
                 similarities(tick + 2)
-            if is_pair(tick - LAG - 1):
-                read_out(tick - LAG - 1)
+            if is_pair(tick - LAG - 1) and (tick - LAG - 1) % QUAD == QUAD - 1:
+                read_out((tick - LAG - 1) // QUAD)
+            if is_pair(tick - LAG):
+                normalise(tick - LAG)
+            if is_pair(tick - LAG + 2):
+                normalise_before_transposes(tick - LAG + 2)
+            if is_pair(tick - LAG + 1):
+                exemplars_to_partitions(tick - LAG + 1)
             if is_pair(tick - PAIRS_PER_TILE - 1) and (tick - 1) % PAIRS_PER_TILE == 0:
                 i = (tick - 1) // PAIRS_PER_TILE - 1
                 spread_flipped[i] = reciprocal_of_row_sum(i)
-            if is_pair(tick - LAG + 1):
-                exemplars_to_partitions(tick - LAG + 1)

@@ -27,6 +27,7 @@ QUAD = 2
 R_PIECES = 4
 SCALAR_EVERY = 8
 LAG = PAIRS_PER_TILE + 3
+FIRST_TICK = -5
 
 
 def tile_minerva_pa_kernel(tc, f_norm, e_norm, ex_class_reps, out):
@@ -34,7 +35,7 @@ def tile_minerva_pa_kernel(tc, f_norm, e_norm, ex_class_reps, out):
     with (
         tc.tile_pool(name="keep", bufs=1) as keep,
         tc.tile_pool(name="raw", bufs=8) as raw_pool,
-        tc.tile_pool(name="stage", bufs=3) as stage,
+        tc.tile_pool(name="stage", bufs=4) as stage,
         tc.tile_pool(name="cubes", bufs=LAG + 1) as cubes,
         tc.tile_pool(name="small", bufs=3) as small,
         tc.psum_pool(name="psum_s", bufs=2 * PAIR) as psum_s,
@@ -107,13 +108,33 @@ def tile_minerva_pa_kernel(tc, f_norm, e_norm, ex_class_reps, out):
             cols = slice(first, first + width)
             nc.vector.quantize_mx(out=codes[:, cols].bitcast(FP8X4), scales=scales[:, cols], in_=grouped[:])
 
-        def prepare_class_reps(g):
+        def exemplars_side_by_side(raw):
             grouped = stage.tile([P, PACK * LABELS * PACK], BF16, tag="grouped", align_bytes=64)
-            nc.vector.tensor_copy(
+            nc.gpsimd.tensor_scalar(
                 out=grouped[:].rearrange("p (c n t) -> p c n t", c=PACK, t=PACK),
-                in_=r_raw[g][:].rearrange("p (c t n) -> p c n t", c=PACK, t=PACK),
+                in0=raw[:].rearrange("p (c t n) -> p c n t", c=PACK, t=PACK),
+                scalar1=1.0,
+                scalar2=0.0,
+                op0=ALU.mult,
+                op1=ALU.add,
             )
             return grouped
+
+        operands = [(f_raw[0], features_to_partitions, f_codes, f_scales, 0)]
+        for c in range(PASSES):
+            operands.append((e_raw[c], features_to_partitions, e_codes, e_scales, c * K_PASS))
+        operands.append((f_raw[1], features_to_partitions, f_codes, f_scales, K_PASS))
+        for g in range(R_PIECES):
+            operands.append((r_raw[g], exemplars_side_by_side, r_codes, r_scales, g * K_PASS))
+        laid_out = {}
+
+        def lay_out(n):
+            if n < len(operands):
+                laid_out[n] = operands[n][1](operands[n][0])
+
+        def quantise_operand(n):
+            if 0 <= n < len(operands):
+                quantise(laid_out[n], operands[n][2], operands[n][3], operands[n][4], K_PASS)
 
         s_banks, squares, a_pairs, abs_sums, totals, recips, recip_rows, flips, p_groups, echoes = (
             {}, {}, {}, {}, {}, {}, {}, {}, {}, {},
@@ -123,6 +144,8 @@ def tile_minerva_pa_kernel(tc, f_norm, e_norm, ex_class_reps, out):
             return 0 <= j < N_PAIRS
 
         def scalar_way(j, cc):
+            if j + LAG >= N_PAIRS:
+                return cc == PAIR - 1
             return (j * PAIR + cc) % SCALAR_EVERY == SCALAR_EVERY - 1
 
         def similarities(j):
@@ -254,28 +277,19 @@ def tile_minerva_pa_kernel(tc, f_norm, e_norm, ex_class_reps, out):
                 nc.scalar.copy(out=result[:], in_=echoes[i][:])
                 nc.sync.dma_start(out=out[i * P : (i + 1) * P, :], in_=result[:])
 
-        grouped = features_to_partitions(f_raw[0])
-        quantise(grouped, f_codes, f_scales, 0, K_PASS)
         spread_flipped = {}
-        for tick in range(-3, N_PAIRS + LAG + 1):
-            prepared = []
-            if tick + 3 < PAIRS_PER_TILE:
-                for c in range((tick + 3) * PAIR, (tick + 4) * PAIR):
-                    prepared.append((features_to_partitions(e_raw[c]), e_codes, e_scales, c * K_PASS))
-            elif tick + 3 == PAIRS_PER_TILE:
-                prepared.append((features_to_partitions(f_raw[1]), f_codes, f_scales, K_PASS))
-            elif tick + 3 <= PAIRS_PER_TILE + R_PIECES:
-                g = tick + 3 - PAIRS_PER_TILE - 1
-                prepared.append((prepare_class_reps(g), r_codes, r_scales, g * K_PASS))
-
+        for tick in range(FIRST_TICK, N_PAIRS + LAG + 1):
+            n = 2 * (tick - FIRST_TICK)
             if is_pair(tick + 1):
                 square(tick + 1)
-            if is_pair(tick - 1):
-                sum_of_abs(tick - 1)
             if is_pair(tick):
                 cube(tick)
-            for grouped, codes, scales, first in prepared:
-                quantise(grouped, codes, scales, first, K_PASS)
+            quantise_operand(n - 2)
+            lay_out(n)
+            if is_pair(tick - 1):
+                sum_of_abs(tick - 1)
+            quantise_operand(n - 1)
+            lay_out(n + 1)
             if is_pair(tick - PAIRS_PER_TILE - 2) and (tick - 2) % PAIRS_PER_TILE == 0:
                 i = (tick - 2) // PAIRS_PER_TILE - 1
                 keep_reciprocal_row(i, spread_flipped[i])
@@ -285,9 +299,8 @@ def tile_minerva_pa_kernel(tc, f_norm, e_norm, ex_class_reps, out):
                 read_out((tick - LAG - 1) // QUAD)
             if is_pair(tick - LAG):
                 normalise(tick - LAG)
-            if is_pair(tick - LAG + 2):
-                normalise_before_transposes(tick - LAG + 2)
             if is_pair(tick - LAG + 1):
+                normalise_before_transposes(tick - LAG + 1)
                 exemplars_to_partitions(tick - LAG + 1)
             if is_pair(tick - PAIRS_PER_TILE - 1) and (tick - 1) % PAIRS_PER_TILE == 0:
                 i = (tick - 1) // PAIRS_PER_TILE - 1

@@ -22,11 +22,11 @@ PASSES = EXEMPLARS // K_PASS
 PAIR = 2
 PAIR_COLS = PAIR * K_PASS
 PAIRS_PER_TILE = PASSES // PAIR
+PAIR_WORDS = PAIR_COLS // 2
 N_PAIRS = Q_TILES * PAIRS_PER_TILE
 QUAD = 2
 R_PIECES = 4
-SCALAR_EVERY = 8
-LAG = PAIRS_PER_TILE + 3
+LAG = PAIRS_PER_TILE + 1
 FIRST_TICK = -5
 
 
@@ -36,7 +36,7 @@ def tile_minerva_pa_kernel(tc, f_norm, e_norm, ex_class_reps, out):
         tc.tile_pool(name="keep", bufs=1) as keep,
         tc.tile_pool(name="raw", bufs=8) as raw_pool,
         tc.tile_pool(name="stage", bufs=4) as stage,
-        tc.tile_pool(name="cubes", bufs=LAG + 1) as cubes,
+        tc.tile_pool(name="cubes", bufs=LAG + 2) as cubes,
         tc.tile_pool(name="small", bufs=3) as small,
         tc.psum_pool(name="psum_s", bufs=2 * PAIR) as psum_s,
         tc.psum_pool(name="psum_flip", bufs=3) as psum_flip,
@@ -75,8 +75,6 @@ def tile_minerva_pa_kernel(tc, f_norm, e_norm, ex_class_reps, out):
 
         ident = keep.tile([P, P], F32)
         make_identity(nc, ident[:])
-        ones = keep.tile([P, P], F32)
-        nc.vector.memset(ones[:], 1.0)
 
         f_codes = keep.tile([P, QUERIES], U32, align_bytes=64)
         f_scales = keep.tile([P, QUERIES], U8, align_bytes=64)
@@ -86,18 +84,22 @@ def tile_minerva_pa_kernel(tc, f_norm, e_norm, ex_class_reps, out):
         r_scales = keep.tile([P, PASSES * LABELS], U8, align_bytes=64)
         abs_out = keep.tile([P, PAIR_COLS], BF16)
 
-        def features_to_partitions(raw):
+        def features_to_partitions(raw, neighbours):
             words = raw[:].bitcast(F32)
             grouped = stage.tile([P, K_PASS * PACK], BF16, tag="grouped", align_bytes=64)
-            grouped_words = grouped[:].bitcast(F32).rearrange("p (j r u) -> p j r u", j=PACK, u=2)
             for half in range(2):
                 flipped = psum_flip.tile([P, PACK, P], F32, tag="flipped")
                 for j in range(2):
                     for u in range(2):
                         first = (2 * half + j) * (FEATURES // 2) + u * P
                         nc.tensor.transpose(flipped[:, 2 * j + u, :], words[:, first : first + P], ident[:])
-                source = flipped[:].rearrange("p (j u) r -> p j r u", u=2)
-                target = grouped_words[:, 2 * half : 2 * half + 2, :, :]
+                target = grouped[:].bitcast(F32)[:, half * K_PASS : (half + 1) * K_PASS]
+                if neighbours:
+                    target = target.rearrange("p (r j u) -> p r j u", j=2, u=2)
+                    source = flipped[:].rearrange("p (j u) r -> p r j u", u=2)
+                else:
+                    target = target.rearrange("p (j r u) -> p j r u", j=2, u=2)
+                    source = flipped[:].rearrange("p (j u) r -> p j r u", u=2)
                 if half == 0:
                     nc.scalar.copy(out=target, in_=source)
                 else:
@@ -120,10 +122,16 @@ def tile_minerva_pa_kernel(tc, f_norm, e_norm, ex_class_reps, out):
             )
             return grouped
 
-        operands = [(f_raw[0], features_to_partitions, f_codes, f_scales, 0)]
+        def queries_laid_out(raw):
+            return features_to_partitions(raw, False)
+
+        def exemplars_laid_out(raw):
+            return features_to_partitions(raw, True)
+
+        operands = [(f_raw[0], queries_laid_out, f_codes, f_scales, 0)]
         for c in range(PASSES):
-            operands.append((e_raw[c], features_to_partitions, e_codes, e_scales, c * K_PASS))
-        operands.append((f_raw[1], features_to_partitions, f_codes, f_scales, K_PASS))
+            operands.append((e_raw[c], exemplars_laid_out, e_codes, e_scales, c * K_PASS))
+        operands.append((f_raw[1], queries_laid_out, f_codes, f_scales, K_PASS))
         for g in range(R_PIECES):
             operands.append((r_raw[g], exemplars_side_by_side, r_codes, r_scales, g * K_PASS))
         laid_out = {}
@@ -136,17 +144,12 @@ def tile_minerva_pa_kernel(tc, f_norm, e_norm, ex_class_reps, out):
             if 0 <= n < len(operands):
                 quantise(laid_out[n], operands[n][2], operands[n][3], operands[n][4], K_PASS)
 
-        s_banks, squares, a_pairs, abs_sums, totals, recips, recip_rows, flips, p_groups, echoes = (
+        s_banks, squares, a_pairs, abs_sums, totals, recips, p_pairs, flips, p_groups, echoes = (
             {}, {}, {}, {}, {}, {}, {}, {}, {}, {},
         )
 
         def is_pair(j):
             return 0 <= j < N_PAIRS
-
-        def scalar_way(j, cc):
-            if j + LAG >= N_PAIRS:
-                return cc == PAIR - 1
-            return (j * PAIR + cc) % SCALAR_EVERY == SCALAR_EVERY - 1
 
         def similarities(j):
             i, pair = divmod(j, PAIRS_PER_TILE)
@@ -203,52 +206,36 @@ def tile_minerva_pa_kernel(tc, f_norm, e_norm, ex_class_reps, out):
             nc.vector.tensor_scalar_max(out=recip[:], in0=totals[i][:], scalar1=EPS)
             nc.vector.reciprocal(out=recip[:], in_=recip[:])
             recips[i] = recip
-            spread = small.tile([P, P], F32, tag="spread")
-            nc.scalar.activation(out=spread[:], in_=ones[:], func=ACT.Copy, scale=recip[:, 0:1])
-            flipped = psum_flip.tile([P, PACK, P], F32, tag="flipped")
-            nc.tensor.transpose(flipped[:, 0, :], spread[:], ident[:])
-            return flipped
-
-        def keep_reciprocal_row(i, flipped):
-            recip_row = small.tile([P, P], F32, tag="recip_row")
-            nc.scalar.copy(out=recip_row[:], in_=flipped[:, 0, :])
-            recip_rows[i] = recip_row
-
-        def normalise_before_transposes(j):
-            i = j // PAIRS_PER_TILE
-            for cc in range(PAIR):
-                if scalar_way(j, cc):
-                    a_pass = a_pairs[j][:, cc * K_PASS : (cc + 1) * K_PASS]
-                    nc.gpsimd.tensor_scalar(
-                        out=a_pass, in0=a_pass, scalar1=recips[i][:, 0:1], scalar2=0.0, op0=ALU.mult, op1=ALU.add
-                    )
-
-        def exemplars_to_partitions(j):
-            for cc in range(PAIR):
-                flipped = psum_flip.tile([P, PACK, P], F32, tag="flipped")
-                for t in range(PACK):
-                    first = cc * K_PASS + t * P
-                    nc.tensor.transpose(flipped[:, t, :], a_pairs[j][:, first : first + P], ident[:])
-                flips[j, cc] = flipped
 
         def normalise(j):
-            i = j // PAIRS_PER_TILE
+            p_pair = stage.tile([P, PAIR_COLS], BF16, tag="p_pair")
+            nc.gpsimd.tensor_scalar(
+                out=p_pair[:],
+                in0=a_pairs[j][:],
+                scalar1=recips[j // PAIRS_PER_TILE][:, 0:1],
+                scalar2=0.0,
+                op0=ALU.mult,
+                op1=ALU.add,
+            )
+            p_pairs[j] = p_pair
+
+        def exemplars_to_partitions(j):
+            words = p_pairs[j][:].bitcast(F32)
+            flipped = psum_flip.tile([P, PACK, P], F32, tag="flipped")
+            for block in range(2 * PAIR):
+                nc.tensor.transpose(flipped[:, block, :], words[:, block * P : (block + 1) * P], ident[:])
+            flips[j] = flipped
+
+        def side_by_side(j):
             if j % QUAD == 0:
                 p_group = stage.tile([P, QUAD * PAIR * P * PACK], BF16, tag="p_group", align_bytes=64)
                 p_groups[j // QUAD] = p_group
-            for cc in range(PAIR):
-                first = ((j % QUAD) * PAIR + cc) * K_PASS
-                target = p_groups[j // QUAD][:, first : first + K_PASS].rearrange("p (q t) -> p q t", t=PACK)
-                source = flips[j, cc][:].rearrange("p t q -> p q t")
-                if scalar_way(j, cc):
-                    nc.scalar.copy(out=target, in_=source)
-                else:
-                    nc.vector.tensor_tensor(
-                        out=target,
-                        in0=source,
-                        in1=recip_rows[i][:].unsqueeze(2).to_broadcast([P, P, PACK]),
-                        op=ALU.mult,
-                    )
+            first = (j % QUAD) * PAIR_WORDS
+            target = p_groups[j // QUAD][:].bitcast(F32)[:, first : first + PAIR_WORDS]
+            nc.vector.tensor_copy(
+                out=target.rearrange("p (c q u) -> p c q u", c=PAIR, u=2),
+                in_=flips[j][:].rearrange("p (c u) q -> p c q u", u=2),
+            )
 
         def read_out(quad):
             passes = QUAD * PAIR
@@ -277,8 +264,7 @@ def tile_minerva_pa_kernel(tc, f_norm, e_norm, ex_class_reps, out):
                 nc.scalar.copy(out=result[:], in_=echoes[i][:])
                 nc.sync.dma_start(out=out[i * P : (i + 1) * P, :], in_=result[:])
 
-        spread_flipped = {}
-        for tick in range(FIRST_TICK, N_PAIRS + LAG + 1):
+        for tick in range(FIRST_TICK, N_PAIRS + LAG + 3):
             n = 2 * (tick - FIRST_TICK)
             if is_pair(tick + 1):
                 square(tick + 1)
@@ -290,18 +276,14 @@ def tile_minerva_pa_kernel(tc, f_norm, e_norm, ex_class_reps, out):
                 sum_of_abs(tick - 1)
             quantise_operand(n - 1)
             lay_out(n + 1)
-            if is_pair(tick - PAIRS_PER_TILE - 2) and (tick - 2) % PAIRS_PER_TILE == 0:
-                i = (tick - 2) // PAIRS_PER_TILE - 1
-                keep_reciprocal_row(i, spread_flipped[i])
-            if is_pair(tick + 2):
-                similarities(tick + 2)
-            if is_pair(tick - LAG - 1) and (tick - LAG - 1) % QUAD == QUAD - 1:
-                read_out((tick - LAG - 1) // QUAD)
             if is_pair(tick - LAG):
                 normalise(tick - LAG)
-            if is_pair(tick - LAG + 1):
-                normalise_before_transposes(tick - LAG + 1)
-                exemplars_to_partitions(tick - LAG + 1)
-            if is_pair(tick - PAIRS_PER_TILE - 1) and (tick - 1) % PAIRS_PER_TILE == 0:
-                i = (tick - 1) // PAIRS_PER_TILE - 1
-                spread_flipped[i] = reciprocal_of_row_sum(i)
+            if is_pair(tick + 2):
+                similarities(tick + 2)
+            if is_pair(tick - LAG - 2) and (tick - LAG - 2) % QUAD == QUAD - 1:
+                read_out((tick - LAG - 2) // QUAD)
+            if is_pair(tick - LAG - 1):
+                exemplars_to_partitions(tick - LAG - 1)
+                side_by_side(tick - LAG - 1)
+            if is_pair(tick - 1) and tick % PAIRS_PER_TILE == 0:
+                reciprocal_of_row_sum(tick // PAIRS_PER_TILE - 1)

@@ -264,7 +264,7 @@ def tile_minerva_pa_kernel(tc, f_norm, e_norm, ex_class_reps, out):
                 nc.scalar.copy(out=result[:], in_=echoes[i][:])
                 nc.sync.dma_start(out=out[i * P : (i + 1) * P, :], in_=result[:])
 
-        for tick in range(FIRST_TICK, N_PAIRS + LAG + 3):
+        for tick in range(FIRST_TICK, N_PAIRS + LAG + 4):
             n = 2 * (tick - FIRST_TICK)
             if is_pair(tick + 1):
                 square(tick + 1)
@@ -276,14 +276,15 @@ def tile_minerva_pa_kernel(tc, f_norm, e_norm, ex_class_reps, out):
                 sum_of_abs(tick - 1)
             quantise_operand(n - 1)
             lay_out(n + 1)
+            if is_pair(tick - LAG) and tick % PAIRS_PER_TILE == LAG % PAIRS_PER_TILE:
+                reciprocal_of_row_sum((tick - LAG) // PAIRS_PER_TILE)
             if is_pair(tick - LAG):
                 normalise(tick - LAG)
             if is_pair(tick + 2):
                 similarities(tick + 2)
-            if is_pair(tick - LAG - 2) and (tick - LAG - 2) % QUAD == QUAD - 1:
-                read_out((tick - LAG - 2) // QUAD)
+            if is_pair(tick - LAG - 3) and (tick - LAG - 3) % QUAD == QUAD - 1:
+                read_out((tick - LAG - 3) // QUAD)
+            if is_pair(tick - LAG - 2):
+                side_by_side(tick - LAG - 2)
             if is_pair(tick - LAG - 1):
                 exemplars_to_partitions(tick - LAG - 1)
-                side_by_side(tick - LAG - 1)
-            if is_pair(tick - 1) and tick % PAIRS_PER_TILE == 0:
-                reciprocal_of_row_sum(tick // PAIRS_PER_TILE - 1)

@@ -24,10 +24,12 @@ PAIR_COLS = PAIR * K_PASS
 PAIRS_PER_TILE = PASSES // PAIR
 PAIR_WORDS = PAIR_COLS // 2
 N_PAIRS = Q_TILES * PAIRS_PER_TILE
+LAST_TILE = N_PAIRS - PAIRS_PER_TILE
 QUAD = 2
 R_PIECES = 4
 LAG = PAIRS_PER_TILE + 1
-FIRST_TICK = -5
+FIRST_TICK = -3
+GPSIMD_PAIRS = (1, 3, 5, 7)
 
 
 def tile_minerva_pa_kernel(tc, f_norm, e_norm, ex_class_reps, out):
@@ -70,8 +72,8 @@ def tile_minerva_pa_kernel(tc, f_norm, e_norm, ex_class_reps, out):
 
         f_raw = [load_queries(0)]
         e_raw = [load_exemplars(c) for c in range(PASSES)]
-        f_raw.append(load_queries(1))
         r_raw = [load_class_reps(g) for g in range(R_PIECES)]
+        f_raw.append(load_queries(1))
 
         ident = keep.tile([P, P], F32)
         make_identity(nc, ident[:])
@@ -84,7 +86,7 @@ def tile_minerva_pa_kernel(tc, f_norm, e_norm, ex_class_reps, out):
         r_scales = keep.tile([P, PASSES * LABELS], U8, align_bytes=64)
         abs_out = keep.tile([P, PAIR_COLS], BF16)
 
-        def features_to_partitions(raw, neighbours):
+        def features_to_partitions(raw, neighbours, tick):
             words = raw[:].bitcast(F32)
             grouped = stage.tile([P, K_PASS * PACK], BF16, tag="grouped", align_bytes=64)
             for half in range(2):
@@ -100,7 +102,7 @@ def tile_minerva_pa_kernel(tc, f_norm, e_norm, ex_class_reps, out):
                 else:
                     target = target.rearrange("p (j r u) -> p j r u", j=2, u=2)
                     source = flipped[:].rearrange("p (j u) r -> p j r u", u=2)
-                if half == 0:
+                if half == 0 or tick < 1:
                     nc.scalar.copy(out=target, in_=source)
                 else:
                     nc.vector.tensor_copy(out=target, in_=source)
@@ -110,40 +112,45 @@ def tile_minerva_pa_kernel(tc, f_norm, e_norm, ex_class_reps, out):
             cols = slice(first, first + width)
             nc.vector.quantize_mx(out=codes[:, cols].bitcast(FP8X4), scales=scales[:, cols], in_=grouped[:])
 
-        def exemplars_side_by_side(raw):
+        def exemplars_side_by_side(raw, tick):
             grouped = stage.tile([P, PACK * LABELS * PACK], BF16, tag="grouped", align_bytes=64)
-            nc.gpsimd.tensor_scalar(
+            nc.vector.tensor_copy(
                 out=grouped[:].rearrange("p (c n t) -> p c n t", c=PACK, t=PACK),
-                in0=raw[:].rearrange("p (c t n) -> p c n t", c=PACK, t=PACK),
-                scalar1=1.0,
-                scalar2=0.0,
-                op0=ALU.mult,
-                op1=ALU.add,
+                in_=raw[:].rearrange("p (c t n) -> p c n t", c=PACK, t=PACK),
             )
             return grouped
 
-        def queries_laid_out(raw):
-            return features_to_partitions(raw, False)
+        def queries_laid_out(raw, tick):
+            return features_to_partitions(raw, False, tick)
 
-        def exemplars_laid_out(raw):
-            return features_to_partitions(raw, True)
+        def exemplars_laid_out(raw, tick):
+            return features_to_partitions(raw, True, tick)
 
         operands = [(f_raw[0], queries_laid_out, f_codes, f_scales, 0)]
         for c in range(PASSES):
             operands.append((e_raw[c], exemplars_laid_out, e_codes, e_scales, c * K_PASS))
-        operands.append((f_raw[1], queries_laid_out, f_codes, f_scales, K_PASS))
         for g in range(R_PIECES):
             operands.append((r_raw[g], exemplars_side_by_side, r_codes, r_scales, g * K_PASS))
+        operands.append((f_raw[1], queries_laid_out, f_codes, f_scales, K_PASS))
+        by_tick = {FIRST_TICK: operands[: 1 + PAIR]}
+        for j in range(1, PAIRS_PER_TILE):
+            by_tick[FIRST_TICK + j] = operands[1 + PAIR * j : 1 + PAIR * (j + 1)]
+        for k in range(1 + PASSES, len(operands)):
+            by_tick[FIRST_TICK + PAIRS_PER_TILE + k - 1 - PASSES] = operands[k : k + 1]
+
+        def lay_out_and_quantise(tick):
+            wait = 1 if tick <= FIRST_TICK + PAIRS_PER_TILE else 3
+            before = laid_out.pop(tick - wait, [])
+            now = by_tick.get(tick, [])
+            laid_out[tick] = []
+            for m in range(max(len(before), len(now))):
+                if m < len(before):
+                    grouped, operand = before[m]
+                    quantise(grouped, operand[2], operand[3], operand[4], K_PASS)
+                if m < len(now):
+                    laid_out[tick].append((now[m][1](now[m][0], tick), now[m]))
+
         laid_out = {}
-
-        def lay_out(n):
-            if n < len(operands):
-                laid_out[n] = operands[n][1](operands[n][0])
-
-        def quantise_operand(n):
-            if 0 <= n < len(operands):
-                quantise(laid_out[n], operands[n][2], operands[n][3], operands[n][4], K_PASS)
-
         s_banks, squares, a_pairs, abs_sums, totals, recips, p_pairs, flips, p_groups, echoes = (
             {}, {}, {}, {}, {}, {}, {}, {}, {}, {},
         )
@@ -189,11 +196,15 @@ def tile_minerva_pa_kernel(tc, f_norm, e_norm, ex_class_reps, out):
         def sum_of_abs(j):
             i, pair = divmod(j, PAIRS_PER_TILE)
             if pair == 0:
-                abs_sum = small.tile([P, PAIRS_PER_TILE], F32, tag="abs_sum")
-                abs_sums[i] = abs_sum
-            nc.scalar.activation(
-                out=abs_out[:], in_=a_pairs[j][:], func=ACT.Abs, accum_out=abs_sums[i][:, pair : pair + 1]
-            )
+                abs_columns = small.tile([P, PAIRS_PER_TILE], F32, tag="abs_columns")
+                abs_sums[i] = abs_columns
+            abs_sum = abs_sums[i][:, pair : pair + 1]
+            if j == N_PAIRS - 1:
+                nc.vector.tensor_reduce(
+                    out=abs_sum, in_=a_pairs[j][:], axis=mybir.AxisListType.X, op=ALU.add, apply_absolute_value=True
+                )
+            else:
+                nc.scalar.activation(out=abs_out[:], in_=a_pairs[j][:], func=ACT.Abs, accum_out=abs_sum)
             if pair == PAIRS_PER_TILE - 1:
                 total = small.tile([P, 1], F32, tag="total")
                 nc.scalar.activation(
@@ -201,22 +212,26 @@ def tile_minerva_pa_kernel(tc, f_norm, e_norm, ex_class_reps, out):
                 )
                 totals[i] = total
 
+        def limit_row_sum(i):
+            limited = small.tile([P, 1], F32, tag="limited")
+            nc.vector.tensor_scalar_max(out=limited[:], in0=totals[i][:], scalar1=EPS)
+            totals[i] = limited
+
         def reciprocal_of_row_sum(i):
             recip = small.tile([P, 1], F32, tag="recip")
-            nc.vector.tensor_scalar_max(out=recip[:], in0=totals[i][:], scalar1=EPS)
-            nc.vector.reciprocal(out=recip[:], in_=recip[:])
+            nc.vector.reciprocal(out=recip[:], in_=totals[i][:])
             recips[i] = recip
 
         def normalise(j):
+            a_pair = a_pairs[j]
+            factor = recips[j // PAIRS_PER_TILE][:, 0:1]
             p_pair = stage.tile([P, PAIR_COLS], BF16, tag="p_pair")
-            nc.gpsimd.tensor_scalar(
-                out=p_pair[:],
-                in0=a_pairs[j][:],
-                scalar1=recips[j // PAIRS_PER_TILE][:, 0:1],
-                scalar2=0.0,
-                op0=ALU.mult,
-                op1=ALU.add,
-            )
+            if j % PAIRS_PER_TILE in GPSIMD_PAIRS and j < LAST_TILE - 2:
+                nc.gpsimd.tensor_scalar(
+                    out=p_pair[:], in0=a_pair[:], scalar1=factor, scalar2=0.0, op0=ALU.mult, op1=ALU.add
+                )
+            else:
+                nc.vector.tensor_scalar_mul(out=p_pair[:], in0=a_pair[:], scalar1=factor)
             p_pairs[j] = p_pair
 
         def exemplars_to_partitions(j):
@@ -232,10 +247,12 @@ def tile_minerva_pa_kernel(tc, f_norm, e_norm, ex_class_reps, out):
                 p_groups[j // QUAD] = p_group
             first = (j % QUAD) * PAIR_WORDS
             target = p_groups[j // QUAD][:].bitcast(F32)[:, first : first + PAIR_WORDS]
-            nc.vector.tensor_copy(
-                out=target.rearrange("p (c q u) -> p c q u", c=PAIR, u=2),
-                in_=flips[j][:].rearrange("p (c u) q -> p c q u", u=2),
-            )
+            target = target.rearrange("p (c q u) -> p c q u", c=PAIR, u=2)
+            source = flips[j][:].rearrange("p (c u) q -> p c q u", u=2)
+            if j + LAG + 4 >= N_PAIRS:
+                nc.scalar.copy(out=target, in_=source)
+            else:
+                nc.vector.tensor_copy(out=target, in_=source)
 
         def read_out(quad):
             passes = QUAD * PAIR
@@ -259,32 +276,58 @@ def tile_minerva_pa_kernel(tc, f_norm, e_norm, ex_class_reps, out):
                     start=(c == 0),
                     stop=(c == PASSES - 1),
                 )
-            if c == PASSES - 1:
-                result = small.tile([P, LABELS], F32, tag="result")
-                nc.scalar.copy(out=result[:], in_=echoes[i][:])
-                nc.sync.dma_start(out=out[i * P : (i + 1) * P, :], in_=result[:])
 
-        for tick in range(FIRST_TICK, N_PAIRS + LAG + 4):
-            n = 2 * (tick - FIRST_TICK)
+        def store(i):
+            result = small.tile([P, LABELS], F32, tag="result")
+            nc.scalar.copy(out=result[:], in_=echoes[i][:])
+            nc.sync.dma_start(out=out[i * P : (i + 1) * P, :], in_=result[:])
+
+        def normalise_tick(j):
+            return j + LAG if j < LAST_TILE else N_PAIRS + (j - LAST_TILE) // 2
+
+        by_normalise_tick = {}
+        for j in range(N_PAIRS):
+            by_normalise_tick.setdefault(normalise_tick(j), []).append(j)
+
+        def first_pairs(tick):
+            return [j // PAIRS_PER_TILE for j in by_normalise_tick.get(tick, []) if j % PAIRS_PER_TILE == 0]
+
+        def normalise_pairs(tick):
+            for j in by_normalise_tick.get(tick, []):
+                normalise(j)
+
+        def turn_pairs(tick):
+            for j in by_normalise_tick.get(tick - 2, []):
+                side_by_side(j)
+            for j in by_normalise_tick.get(tick - 1, []):
+                exemplars_to_partitions(j)
+
+        def finish_pairs(tick):
+            for j in by_normalise_tick.get(tick - 3, []):
+                if j % QUAD == QUAD - 1:
+                    read_out(j // QUAD)
+                if j == LAST_TILE - 1:
+                    store(j // PAIRS_PER_TILE)
+
+        for tick in range(FIRST_TICK, normalise_tick(N_PAIRS - 1) + 5):
             if is_pair(tick + 1):
                 square(tick + 1)
             if is_pair(tick):
                 cube(tick)
-            quantise_operand(n - 2)
-            lay_out(n)
-            if is_pair(tick - 1):
+            lay_out_and_quantise(tick)
+            if is_pair(tick - 1) and tick < N_PAIRS:
                 sum_of_abs(tick - 1)
-            quantise_operand(n - 1)
-            lay_out(n + 1)
-            if is_pair(tick - LAG) and tick % PAIRS_PER_TILE == LAG % PAIRS_PER_TILE:
-                reciprocal_of_row_sum((tick - LAG) // PAIRS_PER_TILE)
-            if is_pair(tick - LAG):
-                normalise(tick - LAG)
+            if tick == N_PAIRS - 1:
+                sum_of_abs(tick)
+            for j in by_normalise_tick.get(tick - 4, []):
+                if j % PAIRS_PER_TILE == PAIRS_PER_TILE - 1 and j != LAST_TILE - 1:
+                    store(j // PAIRS_PER_TILE)
+            for i in first_pairs(tick):
+                limit_row_sum(i)
             if is_pair(tick + 2):
                 similarities(tick + 2)
-            if is_pair(tick - LAG - 3) and (tick - LAG - 3) % QUAD == QUAD - 1:
-                read_out((tick - LAG - 3) // QUAD)
-            if is_pair(tick - LAG - 2):
-                side_by_side(tick - LAG - 2)
-            if is_pair(tick - LAG - 1):
-                exemplars_to_partitions(tick - LAG - 1)
+            turn_pairs(tick)
+            for i in first_pairs(tick):
+                reciprocal_of_row_sum(i)
+            finish_pairs(tick)
+            normalise_pairs(tick)

import concourse.mybir as mybir
from concourse.masks import make_identity

F32 = mybir.dt.float32
BF16 = mybir.dt.bfloat16
U32 = mybir.dt.uint32
U8 = mybir.dt.uint8
FP8X4 = mybir.dt.float8_e4m3fn_x4
ACT = mybir.ActivationFunctionType
ALU = mybir.AluOpType

P = 128
PACK = 4
K_PASS = P * PACK

QUERIES, FEATURES, EXEMPLARS, LABELS = 1024, 512, 8192, 128
EPS = 1e-12
FLOPS = 2 * QUERIES * EXEMPLARS * (FEATURES + LABELS)

Q_TILES = QUERIES // P
PASSES = EXEMPLARS // K_PASS
PAIR = 2
PAIR_COLS = PAIR * K_PASS
PAIRS_PER_TILE = PASSES // PAIR
PAIR_WORDS = PAIR_COLS // 2
N_PAIRS = Q_TILES * PAIRS_PER_TILE
LAST_TILE = N_PAIRS - PAIRS_PER_TILE
QUAD = 2
R_PIECES = 4
LAG = PAIRS_PER_TILE + 1
FIRST_TICK = -3
GPSIMD_PAIRS = (1, 3, 5, 7)


def tile_minerva_pa_kernel(tc, f_norm, e_norm, ex_class_reps, out):
    nc = tc.nc
    with (
        tc.tile_pool(name="keep", bufs=1) as keep,
        tc.tile_pool(name="raw", bufs=8) as raw_pool,
        tc.tile_pool(name="stage", bufs=4) as stage,
        tc.tile_pool(name="cubes", bufs=LAG + 2) as cubes,
        tc.tile_pool(name="small", bufs=3) as small,
        tc.psum_pool(name="psum_s", bufs=2 * PAIR) as psum_s,
        tc.psum_pool(name="psum_flip", bufs=3) as psum_flip,
        tc.psum_pool(name="psum_echo", bufs=1) as psum_echo,
        tc.manual_schedule(),
    ):
        def load_queries(h):
            raw = raw_pool.tile([P, PACK * FEATURES], BF16, tag="raw")
            nc.sync.dma_start(
                out=raw[:].rearrange("p (j k) -> p j k", j=PACK),
                in_=f_norm[h * K_PASS : (h + 1) * K_PASS, :].rearrange("(j p) k -> p j k", p=P),
            )
            return raw

        def load_exemplars(c):
            raw = raw_pool.tile([P, PACK * FEATURES], BF16, tag="raw")
            nc.sync.dma_start(
                out=raw[:],
                in_=e_norm[c * K_PASS : (c + 1) * K_PASS, :].rearrange("(p t) k -> p (t k)", t=PACK),
            )
            return raw

        def load_class_reps(g):
            raw = raw_pool.tile([P, PACK * PACK * LABELS], BF16, tag="raw")
            rows = ex_class_reps[g * PACK * K_PASS : (g + 1) * PACK * K_PASS, :]
            nc.sync.dma_start(
                out=raw[:].rearrange("p (c x) -> p c x", c=PACK),
                in_=rows.rearrange("(c p t) n -> p c (t n)", p=P, t=PACK),
            )
            return raw

        f_raw = [load_queries(0)]
        e_raw = [load_exemplars(c) for c in range(PASSES)]
        r_raw = [load_class_reps(g) for g in range(R_PIECES)]
        f_raw.append(load_queries(1))

        ident = keep.tile([P, P], F32)
        make_identity(nc, ident[:])

        f_codes = keep.tile([P, QUERIES], U32, align_bytes=64)
        f_scales = keep.tile([P, QUERIES], U8, align_bytes=64)
        e_codes = keep.tile([P, EXEMPLARS], U32, align_bytes=64)
        e_scales = keep.tile([P, EXEMPLARS], U8, align_bytes=64)
        r_codes = keep.tile([P, PASSES * LABELS], U32, align_bytes=64)
        r_scales = keep.tile([P, PASSES * LABELS], U8, align_bytes=64)
        abs_out = keep.tile([P, PAIR_COLS], BF16)

        def features_to_partitions(raw, neighbours, tick):
            words = raw[:].bitcast(F32)
            grouped = stage.tile([P, K_PASS * PACK], BF16, tag="grouped", align_bytes=64)
            for half in range(2):
                flipped = psum_flip.tile([P, PACK, P], F32, tag="flipped")
                for j in range(2):
                    for u in range(2):
                        first = (2 * half + j) * (FEATURES // 2) + u * P
                        nc.tensor.transpose(flipped[:, 2 * j + u, :], words[:, first : first + P], ident[:])
                target = grouped[:].bitcast(F32)[:, half * K_PASS : (half + 1) * K_PASS]
                if neighbours:
                    target = target.rearrange("p (r j u) -> p r j u", j=2, u=2)
                    source = flipped[:].rearrange("p (j u) r -> p r j u", u=2)
                else:
                    target = target.rearrange("p (j r u) -> p j r u", j=2, u=2)
                    source = flipped[:].rearrange("p (j u) r -> p j r u", u=2)
                if half == 0 or tick < 1:
                    nc.scalar.copy(out=target, in_=source)
                else:
                    nc.vector.tensor_copy(out=target, in_=source)
            return grouped

        def quantise(grouped, codes, scales, first, width):
            cols = slice(first, first + width)
            nc.vector.quantize_mx(out=codes[:, cols].bitcast(FP8X4), scales=scales[:, cols], in_=grouped[:])

        def exemplars_side_by_side(raw, tick):
            grouped = stage.tile([P, PACK * LABELS * PACK], BF16, tag="grouped", align_bytes=64)
            nc.vector.tensor_copy(
                out=grouped[:].rearrange("p (c n t) -> p c n t", c=PACK, t=PACK),
                in_=raw[:].rearrange("p (c t n) -> p c n t", c=PACK, t=PACK),
            )
            return grouped

        def queries_laid_out(raw, tick):
            return features_to_partitions(raw, False, tick)

        def exemplars_laid_out(raw, tick):
            return features_to_partitions(raw, True, tick)

        operands = [(f_raw[0], queries_laid_out, f_codes, f_scales, 0)]
        for c in range(PASSES):
            operands.append((e_raw[c], exemplars_laid_out, e_codes, e_scales, c * K_PASS))
        for g in range(R_PIECES):
            operands.append((r_raw[g], exemplars_side_by_side, r_codes, r_scales, g * K_PASS))
        operands.append((f_raw[1], queries_laid_out, f_codes, f_scales, K_PASS))
        by_tick = {FIRST_TICK: operands[: 1 + PAIR]}
        for j in range(1, PAIRS_PER_TILE):
            by_tick[FIRST_TICK + j] = operands[1 + PAIR * j : 1 + PAIR * (j + 1)]
        for k in range(1 + PASSES, len(operands)):
            by_tick[FIRST_TICK + PAIRS_PER_TILE + k - 1 - PASSES] = operands[k : k + 1]

        def lay_out_and_quantise(tick):
            wait = 1 if tick <= FIRST_TICK + PAIRS_PER_TILE else 3
            before = laid_out.pop(tick - wait, [])
            now = by_tick.get(tick, [])
            laid_out[tick] = []
            for m in range(max(len(before), len(now))):
                if m < len(before):
                    grouped, operand = before[m]
                    quantise(grouped, operand[2], operand[3], operand[4], K_PASS)
                if m < len(now):
                    laid_out[tick].append((now[m][1](now[m][0], tick), now[m]))

        laid_out = {}
        s_banks, squares, a_pairs, abs_sums, totals, recips, p_pairs, flips, p_groups, echoes = (
            {}, {}, {}, {}, {}, {}, {}, {}, {}, {},
        )

        def is_pair(j):
            return 0 <= j < N_PAIRS

        def similarities(j):
            i, pair = divmod(j, PAIRS_PER_TILE)
            q_cols = slice(i * P, (i + 1) * P)
            for cc in range(PAIR):
                c = pair * PAIR + cc
                e_cols = slice(c * K_PASS, (c + 1) * K_PASS)
                s = psum_s.tile([P, K_PASS], F32, tag="s")
                nc.tensor.matmul_mx(
                    out=s[:],
                    lhsT=f_codes[:, q_cols].bitcast(FP8X4),
                    lhsT_scale=f_scales[:, q_cols],
                    rhs=e_codes[:, e_cols].bitcast(FP8X4),
                    rhs_scale=e_scales[:, e_cols],
                    start=True,
                    stop=True,
                )
                s_banks[j, cc] = s

        def square(j):
            for cc in range(PAIR):
                squared = stage.tile([P, K_PASS], F32, tag="squared", bufs=2 * PAIR)
                nc.scalar.activation(out=squared[:], in_=s_banks[j, cc][:], func=ACT.Square)
                squares[j, cc] = squared

        def cube(j):
            a_pair = cubes.tile([P, PAIR_COLS], F32, tag="a_pair")
            for cc in range(PAIR):
                nc.vector.tensor_tensor(
                    out=a_pair[:, cc * K_PASS : (cc + 1) * K_PASS],
                    in0=s_banks[j, cc][:],
                    in1=squares[j, cc][:],
                    op=ALU.mult,
                )
            a_pairs[j] = a_pair

        def sum_of_abs(j):
            i, pair = divmod(j, PAIRS_PER_TILE)
            if pair == 0:
                abs_columns = small.tile([P, PAIRS_PER_TILE], F32, tag="abs_columns")
                abs_sums[i] = abs_columns
            abs_sum = abs_sums[i][:, pair : pair + 1]
            if j == N_PAIRS - 1:
                nc.vector.tensor_reduce(
                    out=abs_sum, in_=a_pairs[j][:], axis=mybir.AxisListType.X, op=ALU.add, apply_absolute_value=True
                )
            else:
                nc.scalar.activation(out=abs_out[:], in_=a_pairs[j][:], func=ACT.Abs, accum_out=abs_sum)
            if pair == PAIRS_PER_TILE - 1:
                total = small.tile([P, 1], F32, tag="total")
                nc.scalar.activation(
                    out=abs_out[:, 0:PAIRS_PER_TILE], in_=abs_sums[i][:], func=ACT.Copy, accum_out=total[:]
                )
                totals[i] = total

        def limit_row_sum(i):
            limited = small.tile([P, 1], F32, tag="limited")
            nc.vector.tensor_scalar_max(out=limited[:], in0=totals[i][:], scalar1=EPS)
            totals[i] = limited

        def reciprocal_of_row_sum(i):
            recip = small.tile([P, 1], F32, tag="recip")
            nc.vector.reciprocal(out=recip[:], in_=totals[i][:])
            recips[i] = recip

        def normalise(j):
            a_pair = a_pairs[j]
            factor = recips[j // PAIRS_PER_TILE][:, 0:1]
            p_pair = stage.tile([P, PAIR_COLS], BF16, tag="p_pair")
            if j % PAIRS_PER_TILE in GPSIMD_PAIRS and j < LAST_TILE - 2:
                nc.gpsimd.tensor_scalar(
                    out=p_pair[:], in0=a_pair[:], scalar1=factor, scalar2=0.0, op0=ALU.mult, op1=ALU.add
                )
            else:
                nc.vector.tensor_scalar_mul(out=p_pair[:], in0=a_pair[:], scalar1=factor)
            p_pairs[j] = p_pair

        def exemplars_to_partitions(j):
            words = p_pairs[j][:].bitcast(F32)
            flipped = psum_flip.tile([P, PACK, P], F32, tag="flipped")
            for block in range(2 * PAIR):
                nc.tensor.transpose(flipped[:, block, :], words[:, block * P : (block + 1) * P], ident[:])
            flips[j] = flipped

        def side_by_side(j):
            if j % QUAD == 0:
                p_group = stage.tile([P, QUAD * PAIR * P * PACK], BF16, tag="p_group", align_bytes=64)
                p_groups[j // QUAD] = p_group
            first = (j % QUAD) * PAIR_WORDS
            target = p_groups[j // QUAD][:].bitcast(F32)[:, first : first + PAIR_WORDS]
            target = target.rearrange("p (c q u) -> p c q u", c=PAIR, u=2)
            source = flips[j][:].rearrange("p (c u) q -> p c q u", u=2)
            if j + LAG + 4 >= N_PAIRS:
                nc.scalar.copy(out=target, in_=source)
            else:
                nc.vector.tensor_copy(out=target, in_=source)

        def read_out(quad):
            passes = QUAD * PAIR
            i, part = divmod(quad, PASSES // passes)
            p_codes = stage.tile([P, passes * P], U32, tag="p_codes", align_bytes=64)
            p_scales = stage.tile([P, passes * P], U8, tag="p_scales", align_bytes=64)
            quantise(p_groups[quad], p_codes, p_scales, 0, passes * P)
            if part == 0:
                echo = psum_echo.tile([P, LABELS], F32, tag="echo")
                echoes[i] = echo
            for cc in range(passes):
                c = part * passes + cc
                q_cols = slice(cc * P, (cc + 1) * P)
                n_cols = slice(c * LABELS, (c + 1) * LABELS)
                nc.tensor.matmul_mx(
                    out=echoes[i][:],
                    lhsT=p_codes[:, q_cols].bitcast(FP8X4),
                    lhsT_scale=p_scales[:, q_cols],
                    rhs=r_codes[:, n_cols].bitcast(FP8X4),
                    rhs_scale=r_scales[:, n_cols],
                    start=(c == 0),
                    stop=(c == PASSES - 1),
                )

        def store(i):
            result = small.tile([P, LABELS], F32, tag="result")
            nc.scalar.copy(out=result[:], in_=echoes[i][:])
            nc.sync.dma_start(out=out[i * P : (i + 1) * P, :], in_=result[:])

        def normalise_tick(j):
            return j + LAG if j < LAST_TILE else N_PAIRS + (j - LAST_TILE) // 2

        by_normalise_tick = {}
        for j in range(N_PAIRS):
            by_normalise_tick.setdefault(normalise_tick(j), []).append(j)

        def first_pairs(tick):
            return [j // PAIRS_PER_TILE for j in by_normalise_tick.get(tick, []) if j % PAIRS_PER_TILE == 0]

        def normalise_pairs(tick):
            for j in by_normalise_tick.get(tick, []):
                normalise(j)

        def turn_pairs(tick):
            for j in by_normalise_tick.get(tick - 2, []):
                side_by_side(j)
            for j in by_normalise_tick.get(tick - 1, []):
                exemplars_to_partitions(j)

        def finish_pairs(tick):
            for j in by_normalise_tick.get(tick - 3, []):
                if j % QUAD == QUAD - 1:
                    read_out(j // QUAD)
                if j == LAST_TILE - 1:
                    store(j // PAIRS_PER_TILE)

        for tick in range(FIRST_TICK, normalise_tick(N_PAIRS - 1) + 5):
            if is_pair(tick + 1):
                square(tick + 1)
            if is_pair(tick):
                cube(tick)
            lay_out_and_quantise(tick)
            if is_pair(tick - 1) and tick < N_PAIRS:
                sum_of_abs(tick - 1)
            if tick == N_PAIRS - 1:
                sum_of_abs(tick)
            for j in by_normalise_tick.get(tick - 4, []):
                if j % PAIRS_PER_TILE == PAIRS_PER_TILE - 1 and j != LAST_TILE - 1:
                    store(j // PAIRS_PER_TILE)
            for i in first_pairs(tick):
                limit_row_sum(i)
            if is_pair(tick + 2):
                similarities(tick + 2)
            turn_pairs(tick)
            for i in first_pairs(tick):
                reciprocal_of_row_sum(i)
            finish_pairs(tick)
            normalise_pairs(tick)
